import numpy as np
import ml_dtypes


def mxq(x, axis, fmt="e4m3"):
    dtype, down = {"e4m3": (ml_dtypes.float8_e4m3fn, 7), "e5m2": (ml_dtypes.float8_e5m2, 14)}[fmt]
    v = np.moveaxis(np.asarray(x, np.float32).astype(ml_dtypes.bfloat16).astype(np.float64), axis, -1)
    blocks = v.reshape(v.shape[:-1] + (-1, 32))
    amax = np.abs(blocks).max(-1, keepdims=True)
    byte = np.maximum(np.where(amax > 0, np.frexp(amax)[1] - 1 + 127, 0) - down, 1)
    scale = np.exp2(byte - 127.0)
    codes = (blocks / scale).astype(np.float32).astype(dtype).astype(np.float64)
    return np.moveaxis((codes * scale).reshape(v.shape), -1, axis)


BF16 = ml_dtypes.bfloat16


def bf(x):
    return np.asarray(x, np.float32).astype(BF16)


def f64(x):
    return np.asarray(x).astype(np.float64)


B, DIM, Z = 16, 512, 128

TAU = 1.0


def setup_inputs():
    return {"input": bf(np.random.standard_normal((B, DIM, Z)) * 0.25 * np.sqrt(DIM)),
            "scores": bf(np.log(4.0 / DIM) + np.random.uniform(-0.75, 0.75, (B, DIM)))}


def reference(input, scores):
    e = np.exp(f64(scores))
    A = np.abs(e[:, :, None] - e[:, None, :])
    rowsum = A.sum(-1)
    scaling = DIM + 1 - 2.0 * (np.arange(DIM) + 1)
    P_max = scaling[None, :, None] * e[:, None, :] - rowsum[:, None, :]
    P_hat_raw = P_max / TAU
    ex = np.exp(P_hat_raw - P_hat_raw.max(-1, keepdims=True))
    P_hat = ex / ex.sum(-1, keepdims=True)
    out = mxq(P_hat, 2, "e4m3") @ mxq(f64(input), 1, "e4m3")
    return (out, P_hat, P_hat_raw)

@@ -1,0 +1,130 @@
+from contextlib import ExitStack
+
+import concourse.mybir as mybir
+from concourse.masks import make_identity
+
+F32 = mybir.dt.float32
+BF16 = mybir.dt.bfloat16
+I32 = mybir.dt.int32
+U32 = mybir.dt.uint32
+U8 = mybir.dt.uint8
+FP8X4 = mybir.dt.float8_e4m3fn_x4
+ALU = mybir.AluOpType
+ACT = mybir.ActivationFunctionType
+
+B, DIM, Z = 16, 512, 128
+P = 128
+NT = DIM // P
+FLOPS = 2 * B * DIM * DIM * Z
+
+
+def tile_neuralsort_kernel(tc, values, scores, out_0, out_1, out_2):
+    nc = tc.nc
+    with ExitStack() as ctx:
+        const = ctx.enter_context(tc.tile_pool(name="const", bufs=1))
+        work = ctx.enter_context(tc.tile_pool(name="work", bufs=2))
+        small = ctx.enter_context(tc.tile_pool(name="small", bufs=3))
+        psum = ctx.enter_context(tc.psum_pool(name="psum", bufs=1))
+
+        sc = const.tile([P, P], BF16, name="sc")
+        nc.vector.memset(sc[64:128, :], 0.0)
+        nc.sync.dma_start(out=sc[0:64, :], in_=scores.rearrange("b (t q) -> (b t) q", q=P))
+        in_raw = const.tile([P, B, NT, Z], BF16, name="in_raw")
+        vview = values.rearrange("b (t q) z -> q b t z", q=P)
+        for g in range(4):
+            nc.sync.dma_start(out=in_raw[:, 4 * g:4 * g + 4], in_=vview[:, 4 * g:4 * g + 4])
+
+        ident = const.tile([P, P], F32, name="ident")
+        make_identity(nc, ident[:])
+        ns_int = const.tile([P, NT, P], I32, name="ns_int")
+        nc.gpsimd.iota(ns_int[:], pattern=[[2, NT], [8, P]], base=-(DIM - 1), channel_multiplier=0)
+        ns = const.tile([P, DIM], F32, name="ns")
+        nc.vector.tensor_copy(out=ns[:], in_=ns_int[:].rearrange("p a q -> p (a q)"))
+
+        e_rows = const.tile([P, P], F32, name="e_rows")
+        nc.scalar.activation(out=e_rows[:], in_=sc[:], func=ACT.Exp)
+        e_ps = psum.tile([P, DIM], F32, tag="eb", bufs=2, name="e_ps")
+        nc.tensor.transpose(e_ps[:, 0:P], e_rows[:], ident[:])
+        e_col = const.tile([P, B * NT], F32, name="e_col")
+        nc.vector.tensor_copy(out=e_col[:], in_=e_ps[:, 0:B * NT])
+        r_col = const.tile([P, B * NT], F32, name="r_col")
+
+        igr = const.tile([P, B, Z, NT], BF16, name="igr", align_bytes=64)
+        icodes = const.tile([P, B, Z], U32, name="icodes", align_bytes=64)
+        iscales = const.tile([P, B, Z], U8, name="iscales", align_bytes=64)
+        for g in range(4):
+            bs = slice(4 * g, 4 * g + 4)
+            nc.vector.tensor_copy(out=igr[:, bs], in_=in_raw[:, bs].rearrange("p b t z -> p b z t"))
+        for g in range(4):
+            bs = slice(4 * g, 4 * g + 4)
+            nc.vector.quantize_mx(
+                out=icodes[:, bs].rearrange("p b z -> p (b z)").bitcast(FP8X4),
+                scales=iscales[:, bs].rearrange("p b z -> p (b z)"),
+                in_=igr[:, bs].rearrange("p b z t -> p (b z t)"),
+            )
+
+        for b in range(B):
+            eb = psum.tile([P, DIM], F32, tag="eb", bufs=2, name="eb")
+            for t in range(NT):
+                c = b * NT + t
+                nc.tensor.transpose(eb[:, t * P:(t + 1) * P], e_col[:, c:c + 1].to_broadcast([P, P]), ident[:])
+            for t in range(NT):
+                c = b * NT + t
+                junk = work.tile([P, DIM], BF16, tag="junk", name="junk")
+                nc.scalar.activation(out=junk[:], in_=eb[:], func=ACT.Abs, bias=e_col[:, c:c + 1],
+                                     scale=-1.0, accum_out=r_col[:, c:c + 1])
+            nrt = work.tile([P, NT, DIM], F32, tag="nrt", name="nrt")
+            for t in range(NT):
+                c = b * NT + t
+                nc.gpsimd.tensor_scalar(out=nrt[:, t, :], in0=ns[:], scalar1=e_col[:, c:c + 1],
+                                        scalar2=r_col[:, c:c + 1], op0=ALU.mult, op1=ALU.add)
+            raw_sb = work.tile([P, NT, DIM], F32, tag="raw", bufs=3, name="raw_sb")
+            mx = small.tile([P, NT], F32, tag="mx", name="mx")
+            for a in range(NT):
+                rp = psum.tile([P, DIM], F32, tag="rp", bufs=3, name="rp")
+                for t in range(NT):
+                    nc.tensor.transpose(rp[:, t * P:(t + 1) * P], nrt[:, t, a * P:(a + 1) * P], ident[:])
+                nc.vector.tensor_scalar(out=raw_sb[:, a, :], in0=rp[:], scalar1=-1.0, scalar2=None,
+                                        op0=ALU.mult, op1=ALU.max, accum_out=mx[:, a:a + 1])
+            nc.sync.dma_start(out=out_2[b].rearrange("(p a) i -> p (a i)", a=NT),
+                              in_=raw_sb[:].rearrange("p a i -> p (a i)"))
+            nmx = small.tile([P, NT], F32, tag="nmx", name="nmx")
+            nc.vector.tensor_scalar_mul(out=nmx[:], in0=mx[:], scalar1=-1.0)
+            ex = work.tile([P, NT, DIM], F32, tag="ex", name="ex")
+            sm = small.tile([P, NT], F32, tag="sm", name="sm")
+            for a in range(NT):
+                nc.scalar.activation(out=ex[:, a, :], in_=raw_sb[:, a, :], func=ACT.Exp,
+                                     bias=nmx[:, a:a + 1], scale=1.0, accum_out=sm[:, a:a + 1])
+            rinv = small.tile([P, NT], F32, tag="rinv", name="rinv")
+            nc.vector.reciprocal(out=rinv[:], in_=sm[:])
+            ph = work.tile([P, NT, DIM], F32, tag="ph", bufs=3, name="ph")
+            for a in range(NT):
+                nc.vector.tensor_scalar_mul(out=ph[:, a, :], in0=ex[:, a, :], scalar1=rinv[:, a:a + 1])
+            nc.sync.dma_start(out=out_1[b].rearrange("(p a) i -> p (a i)", a=NT),
+                              in_=ph[:].rearrange("p a i -> p (a i)"))
+            gr = work.tile([P, NT, P, NT], BF16, tag="gr", name="gr", align_bytes=64)
+            for a in range(NT):
+                pt = psum.tile([P, NT, P], F32, tag="pt", bufs=2, name="pt")
+                for t in range(NT):
+                    nc.tensor.transpose(pt[:, t, :], ph[:, a, t * P:(t + 1) * P], ident[:])
+                src = pt[:].rearrange("q t p -> q p t")
+                if a < 2 or (a == 2 and b % 2 == 0):
+                    nc.scalar.copy(out=gr[:, a], in_=src)
+                else:
+                    nc.vector.tensor_copy(out=gr[:, a], in_=src)
+            pcodes = work.tile([P, DIM], U32, tag="pcodes", name="pcodes", align_bytes=64)
+            pscales = work.tile([P, DIM], U8, tag="pscales", name="pscales", align_bytes=64)
+            nc.vector.quantize_mx(out=pcodes[:].bitcast(FP8X4), scales=pscales[:],
+                                  in_=gr[:].rearrange("q a p t -> q (a p t)"))
+            op = psum.tile([P, NT, Z], F32, tag="op", bufs=1, name="op")
+            for a in range(NT):
+                nc.tensor.matmul_mx(out=op[:, a, :],
+                                    lhsT=pcodes[:, a * P:(a + 1) * P].bitcast(FP8X4),
+                                    lhsT_scale=pscales[:, a * P:(a + 1) * P],
+                                    rhs=icodes[:, b, :].bitcast(FP8X4),
+                                    rhs_scale=iscales[:, b, :],
+                                    start=True, stop=True)
+            osb = work.tile([P, NT, Z], F32, tag="osb", bufs=3, name="osb")
+            nc.vector.tensor_copy(out=osb[:], in_=op[:])
+            nc.sync.dma_start(out=out_0[b].rearrange("(p a) z -> p (a z)", a=NT),
+                              in_=osb[:].rearrange("p a z -> p (a z)"))

@@ -23,8 +23,9 @@ def tile_neuralsort_kernel(tc, values, scores, out_0, out_1, out_2):
     with ExitStack() as ctx:
         const = ctx.enter_context(tc.tile_pool(name="const", bufs=1))
         work = ctx.enter_context(tc.tile_pool(name="work", bufs=2))
-        small = ctx.enter_context(tc.tile_pool(name="small", bufs=3))
+        small = ctx.enter_context(tc.tile_pool(name="small", bufs=4))
         psum = ctx.enter_context(tc.psum_pool(name="psum", bufs=1))
+        ctx.enter_context(tc.manual_schedule())
 
         sc = const.tile([P, P], BF16, name="sc")
         nc.vector.memset(sc[64:128, :], 0.0)
@@ -52,10 +53,12 @@ def tile_neuralsort_kernel(tc, values, scores, out_0, out_1, out_2):
         igr = const.tile([P, B, Z, NT], BF16, name="igr", align_bytes=64)
         icodes = const.tile([P, B, Z], U32, name="icodes", align_bytes=64)
         iscales = const.tile([P, B, Z], U8, name="iscales", align_bytes=64)
-        for g in range(4):
+
+        def in_regroup(g):
             bs = slice(4 * g, 4 * g + 4)
             nc.vector.tensor_copy(out=igr[:, bs], in_=in_raw[:, bs].rearrange("p b t z -> p b z t"))
-        for g in range(4):
+
+        def in_quant(g):
             bs = slice(4 * g, 4 * g + 4)
             nc.vector.quantize_mx(
                 out=icodes[:, bs].rearrange("p b z -> p (b z)").bitcast(FP8X4),
@@ -63,68 +66,167 @@ def tile_neuralsort_kernel(tc, values, scores, out_0, out_1, out_2):
                 in_=igr[:, bs].rearrange("p b z t -> p (b z t)"),
             )
 
-        for b in range(B):
-            eb = psum.tile([P, DIM], F32, tag="eb", bufs=2, name="eb")
+        T = {}
+
+        def ok(b):
+            return 0 <= b < B
+
+        def eb_pe(b):
+            if not ok(b):
+                return
+            T["eb", b] = psum.tile([P, DIM], F32, tag="eb", bufs=2, name="eb")
             for t in range(NT):
                 c = b * NT + t
-                nc.tensor.transpose(eb[:, t * P:(t + 1) * P], e_col[:, c:c + 1].to_broadcast([P, P]), ident[:])
+                nc.tensor.transpose(T["eb", b][:, t * P:(t + 1) * P], e_col[:, c:c + 1].to_broadcast([P, P]), ident[:])
+
+        def p1_s(b, t):
+            if not ok(b):
+                return
+            c = b * NT + t
+            junk = work.tile([P, DIM], BF16, tag="junk", name="junk")
+            nc.scalar.activation(out=junk[:], in_=T["eb", b][:], func=ACT.Abs, bias=e_col[:, c:c + 1],
+                                 scale=-1.0, accum_out=r_col[:, c:c + 1])
+
+        def rawt_g(b, t):
+            if not ok(b):
+                return
+            if t == 0:
+                T["nrt", b] = work.tile([P, NT, DIM], F32, tag="nrt", bufs=3, name="nrt")
+            c = b * NT + t
+            nc.gpsimd.tensor_scalar(out=T["nrt", b][:, t, :], in0=ns[:], scalar1=e_col[:, c:c + 1],
+                                    scalar2=r_col[:, c:c + 1], op0=ALU.mult, op1=ALU.add)
+
+        def rp_pe(b, a):
+            if not ok(b):
+                return
+            T["rp", b, a] = psum.tile([P, DIM], F32, tag="rp", bufs=3, name="rp")
             for t in range(NT):
-                c = b * NT + t
-                junk = work.tile([P, DIM], BF16, tag="junk", name="junk")
-                nc.scalar.activation(out=junk[:], in_=eb[:], func=ACT.Abs, bias=e_col[:, c:c + 1],
-                                     scale=-1.0, accum_out=r_col[:, c:c + 1])
-            nrt = work.tile([P, NT, DIM], F32, tag="nrt", name="nrt")
-            for t in range(NT):
-                c = b * NT + t
-                nc.gpsimd.tensor_scalar(out=nrt[:, t, :], in0=ns[:], scalar1=e_col[:, c:c + 1],
-                                        scalar2=r_col[:, c:c + 1], op0=ALU.mult, op1=ALU.add)
-            raw_sb = work.tile([P, NT, DIM], F32, tag="raw", bufs=3, name="raw_sb")
-            mx = small.tile([P, NT], F32, tag="mx", name="mx")
-            for a in range(NT):
-                rp = psum.tile([P, DIM], F32, tag="rp", bufs=3, name="rp")
-                for t in range(NT):
-                    nc.tensor.transpose(rp[:, t * P:(t + 1) * P], nrt[:, t, a * P:(a + 1) * P], ident[:])
-                nc.vector.tensor_scalar(out=raw_sb[:, a, :], in0=rp[:], scalar1=-1.0, scalar2=None,
-                                        op0=ALU.mult, op1=ALU.max, accum_out=mx[:, a:a + 1])
+                nc.tensor.transpose(T["rp", b, a][:, t * P:(t + 1) * P], T["nrt", b][:, t, a * P:(a + 1) * P], ident[:])
+
+        def evac_v(b, a):
+            if not ok(b):
+                return
+            if a == 0:
+                T["raw", b] = work.tile([P, NT, DIM], F32, tag="raw", bufs=3, name="raw_sb")
+                T["mx", b] = small.tile([P, NT], F32, tag="mx", name="mx")
+            nc.vector.tensor_scalar(out=T["raw", b][:, a, :], in0=T["rp", b, a][:], scalar1=-1.0, scalar2=None,
+                                    op0=ALU.mult, op1=ALU.max, accum_out=T["mx", b][:, a:a + 1])
+
+        def raw_store(b):
+            if not ok(b):
+                return
             nc.sync.dma_start(out=out_2[b].rearrange("(p a) i -> p (a i)", a=NT),
-                              in_=raw_sb[:].rearrange("p a i -> p (a i)"))
-            nmx = small.tile([P, NT], F32, tag="nmx", name="nmx")
-            nc.vector.tensor_scalar_mul(out=nmx[:], in0=mx[:], scalar1=-1.0)
-            ex = work.tile([P, NT, DIM], F32, tag="ex", name="ex")
-            sm = small.tile([P, NT], F32, tag="sm", name="sm")
-            for a in range(NT):
-                nc.scalar.activation(out=ex[:, a, :], in_=raw_sb[:, a, :], func=ACT.Exp,
-                                     bias=nmx[:, a:a + 1], scale=1.0, accum_out=sm[:, a:a + 1])
-            rinv = small.tile([P, NT], F32, tag="rinv", name="rinv")
-            nc.vector.reciprocal(out=rinv[:], in_=sm[:])
-            ph = work.tile([P, NT, DIM], F32, tag="ph", bufs=3, name="ph")
-            for a in range(NT):
-                nc.vector.tensor_scalar_mul(out=ph[:, a, :], in0=ex[:, a, :], scalar1=rinv[:, a:a + 1])
+                              in_=T["raw", b][:].rearrange("p a i -> p (a i)"))
+
+        def neg_v(b):
+            if not ok(b):
+                return
+            T["nmx", b] = small.tile([P, NT], F32, tag="nmx", name="nmx")
+            nc.vector.tensor_scalar_mul(out=T["nmx", b][:], in0=T["mx", b][:], scalar1=-1.0)
+
+        def exp_s(b, a):
+            if not ok(b):
+                return
+            if a == 0:
+                T["ex", b] = work.tile([P, NT, DIM], F32, tag="ex", bufs=3, name="ex")
+                T["sm", b] = small.tile([P, NT], F32, tag="sm", name="sm")
+            nc.scalar.activation(out=T["ex", b][:, a, :], in_=T["raw", b][:, a, :], func=ACT.Exp,
+                                 bias=T["nmx", b][:, a:a + 1], scale=1.0, accum_out=T["sm", b][:, a:a + 1])
+
+        def recip_v(b):
+            if not ok(b):
+                return
+            T["rinv", b] = small.tile([P, NT], F32, tag="rinv", name="rinv")
+            nc.vector.reciprocal(out=T["rinv", b][:], in_=T["sm", b][:])
+
+        def p5(b, a):
+            if not ok(b):
+                return
+            if a == 0:
+                T["ph", b] = work.tile([P, NT, DIM], F32, tag="ph", bufs=3, name="ph")
+            if a % 2 == 1:
+                nc.gpsimd.tensor_scalar(out=T["ph", b][:, a, :], in0=T["ex", b][:, a, :],
+                                        scalar1=T["rinv", b][:, a:a + 1], scalar2=0.0, op0=ALU.mult, op1=ALU.add)
+            else:
+                nc.vector.tensor_scalar_mul(out=T["ph", b][:, a, :], in0=T["ex", b][:, a, :],
+                                            scalar1=T["rinv", b][:, a:a + 1])
+
+        def ph_store(b):
+            if not ok(b):
+                return
             nc.sync.dma_start(out=out_1[b].rearrange("(p a) i -> p (a i)", a=NT),
-                              in_=ph[:].rearrange("p a i -> p (a i)"))
-            gr = work.tile([P, NT, P, NT], BF16, tag="gr", name="gr", align_bytes=64)
+                              in_=T["ph", b][:].rearrange("p a i -> p (a i)"))
+
+        def pt_pe(b, a):
+            if not ok(b):
+                return
+            T["pt", b, a] = psum.tile([P, NT, P], F32, tag="pt", bufs=2, name="pt")
+            for t in range(NT):
+                nc.tensor.transpose(T["pt", b, a][:, t, :], T["ph", b][:, a, t * P:(t + 1) * P], ident[:])
+
+        def pt_evac(b, a):
+            if not ok(b):
+                return
+            if a == 0:
+                T["gr", b] = work.tile([P, NT, P, NT], BF16, tag="gr", bufs=2, name="gr", align_bytes=64)
+            src = T["pt", b, a][:].rearrange("q t p -> q p t")
+            if a == 0 or (a == 1 and b % 2 == 0):
+                nc.scalar.copy(out=T["gr", b][:, a], in_=src)
+            else:
+                nc.vector.tensor_copy(out=T["gr", b][:, a], in_=src)
+
+        def quant_v(b):
+            if not ok(b):
+                return
+            T["pc", b] = work.tile([P, DIM], U32, tag="pcodes", name="pcodes", align_bytes=64)
+            T["ps", b] = work.tile([P, DIM], U8, tag="pscales", name="pscales", align_bytes=64)
+            nc.vector.quantize_mx(out=T["pc", b][:].bitcast(FP8X4), scales=T["ps", b][:],
+                                  in_=T["gr", b][:].rearrange("q a p t -> q (a p t)"))
+
+        def mx_pe(b):
+            if not ok(b):
+                return
+            T["op", b] = psum.tile([P, NT, Z], F32, tag="op", bufs=1, name="op")
             for a in range(NT):
-                pt = psum.tile([P, NT, P], F32, tag="pt", bufs=2, name="pt")
-                for t in range(NT):
-                    nc.tensor.transpose(pt[:, t, :], ph[:, a, t * P:(t + 1) * P], ident[:])
-                src = pt[:].rearrange("q t p -> q p t")
-                if a < 2 or (a == 2 and b % 2 == 0):
-                    nc.scalar.copy(out=gr[:, a], in_=src)
-                else:
-                    nc.vector.tensor_copy(out=gr[:, a], in_=src)
-            pcodes = work.tile([P, DIM], U32, tag="pcodes", name="pcodes", align_bytes=64)
-            pscales = work.tile([P, DIM], U8, tag="pscales", name="pscales", align_bytes=64)
-            nc.vector.quantize_mx(out=pcodes[:].bitcast(FP8X4), scales=pscales[:],
-                                  in_=gr[:].rearrange("q a p t -> q (a p t)"))
-            op = psum.tile([P, NT, Z], F32, tag="op", bufs=1, name="op")
-            for a in range(NT):
-                nc.tensor.matmul_mx(out=op[:, a, :],
-                                    lhsT=pcodes[:, a * P:(a + 1) * P].bitcast(FP8X4),
-                                    lhsT_scale=pscales[:, a * P:(a + 1) * P],
+                nc.tensor.matmul_mx(out=T["op", b][:, a, :],
+                                    lhsT=T["pc", b][:, a * P:(a + 1) * P].bitcast(FP8X4),
+                                    lhsT_scale=T["ps", b][:, a * P:(a + 1) * P],
                                     rhs=icodes[:, b, :].bitcast(FP8X4),
                                     rhs_scale=iscales[:, b, :],
                                     start=True, stop=True)
+
+        def o_evac(b):
+            if not ok(b):
+                return
             osb = work.tile([P, NT, Z], F32, tag="osb", bufs=3, name="osb")
-            nc.vector.tensor_copy(out=osb[:], in_=op[:])
+            nc.vector.tensor_copy(out=osb[:], in_=T["op", b][:])
             nc.sync.dma_start(out=out_0[b].rearrange("(p a) z -> p (a z)", a=NT),
                               in_=osb[:].rearrange("p a z -> p (a z)"))
+
+        eb_pe(0)
+        for k in range(B + 6):
+            quant_v(k - 5)
+            recip_v(k - 3)
+            eb_pe(k + 1)
+            if k < 4:
+                in_regroup(k)
+            for x in range(NT):
+                if x < 2:
+                    p1_s(k, 2 * x)
+                    rawt_g(k, 2 * x)
+                    p1_s(k, 2 * x + 1)
+                    rawt_g(k, 2 * x + 1)
+                rp_pe(k - 1, x)
+                evac_v(k - 1, x)
+                exp_s(k - 2, x)
+                p5(k - 3, x)
+                pt_pe(k - 4, x)
+                pt_evac(k - 4, x)
+                if x == 1:
+                    mx_pe(k - 5)
+            raw_store(k - 1)
+            ph_store(k - 3)
+            neg_v(k - 1)
+            o_evac(k - 5)
+            if k < 4:
+                in_quant(k)

@@ -27,13 +27,30 @@ def tile_neuralsort_kernel(tc, values, scores, out_0, out_1, out_2):
         psum = ctx.enter_context(tc.psum_pool(name="psum", bufs=1))
         ctx.enter_context(tc.manual_schedule())
 
+        warm = const.tile([P, 1], F32, name="warm")
+        nc.vector.memset(warm[:], 0.0)
+        nc.scalar.activation(out=warm[:], in_=warm[:], func=ACT.Exp)
         sc = const.tile([P, P], BF16, name="sc")
         nc.vector.memset(sc[64:128, :], 0.0)
         nc.sync.dma_start(out=sc[0:64, :], in_=scores.rearrange("b (t q) -> (b t) q", q=P))
+        sb = const.tile([P, B * DIM], BF16, name="sb")
+        sflat = scores.rearrange("b i -> (b i)")
         in_raw = const.tile([P, B, NT, Z], BF16, name="in_raw")
         vview = values.rearrange("b (t q) z -> q b t z", q=P)
-        for g in range(4):
+
+        def sb_load(b0, b1):
+            nc.sync.dma_start(out=sb[:, b0 * DIM:b1 * DIM], in_=sflat[b0 * DIM:b1 * DIM].partition_broadcast(P))
+
+        def in_load(g):
             nc.sync.dma_start(out=in_raw[:, 4 * g:4 * g + 4], in_=vview[:, 4 * g:4 * g + 4])
+
+        sb_load(0, 2)
+        sb_load(2, 8)
+        in_load(0)
+        sb_load(8, 16)
+        in_load(1)
+        in_load(2)
+        in_load(3)
 
         ident = const.tile([P, P], F32, name="ident")
         make_identity(nc, ident[:])
@@ -44,7 +61,7 @@ def tile_neuralsort_kernel(tc, values, scores, out_0, out_1, out_2):
 
         e_rows = const.tile([P, P], F32, name="e_rows")
         nc.scalar.activation(out=e_rows[:], in_=sc[:], func=ACT.Exp)
-        e_ps = psum.tile([P, DIM], F32, tag="eb", bufs=2, name="e_ps")
+        e_ps = psum.tile([P, DIM], F32, tag="pt", bufs=3, name="e_ps")
         nc.tensor.transpose(e_ps[:, 0:P], e_rows[:], ident[:])
         e_col = const.tile([P, B * NT], F32, name="e_col")
         nc.vector.tensor_copy(out=e_col[:], in_=e_ps[:, 0:B * NT])
@@ -71,13 +88,11 @@ def tile_neuralsort_kernel(tc, values, scores, out_0, out_1, out_2):
         def ok(b):
             return 0 <= b < B
 
-        def eb_pe(b):
+        def eb_s(b):
             if not ok(b):
                 return
-            T["eb", b] = psum.tile([P, DIM], F32, tag="eb", bufs=2, name="eb")
-            for t in range(NT):
-                c = b * NT + t
-                nc.tensor.transpose(T["eb", b][:, t * P:(t + 1) * P], e_col[:, c:c + 1].to_broadcast([P, P]), ident[:])
+            T["eb", b] = work.tile([P, DIM], F32, tag="eb", bufs=2, name="eb")
+            nc.scalar.activation(out=T["eb", b][:], in_=sb[:, b * DIM:(b + 1) * DIM], func=ACT.Exp)
 
         def p1_s(b, t):
             if not ok(b):
@@ -99,7 +114,7 @@ def tile_neuralsort_kernel(tc, values, scores, out_0, out_1, out_2):
         def rp_pe(b, a):
             if not ok(b):
                 return
-            T["rp", b, a] = psum.tile([P, DIM], F32, tag="rp", bufs=3, name="rp")
+            T["rp", b, a] = psum.tile([P, DIM], F32, tag="rp", bufs=4, name="rp")
             for t in range(NT):
                 nc.tensor.transpose(T["rp", b, a][:, t * P:(t + 1) * P], T["nrt", b][:, t, a * P:(a + 1) * P], ident[:])
 
@@ -144,7 +159,7 @@ def tile_neuralsort_kernel(tc, values, scores, out_0, out_1, out_2):
                 return
             if a == 0:
                 T["ph", b] = work.tile([P, NT, DIM], F32, tag="ph", bufs=3, name="ph")
-            if a % 2 == 1:
+            if a != 0:
                 nc.gpsimd.tensor_scalar(out=T["ph", b][:, a, :], in0=T["ex", b][:, a, :],
                                         scalar1=T["rinv", b][:, a:a + 1], scalar2=0.0, op0=ALU.mult, op1=ALU.add)
             else:
@@ -160,7 +175,7 @@ def tile_neuralsort_kernel(tc, values, scores, out_0, out_1, out_2):
         def pt_pe(b, a):
             if not ok(b):
                 return
-            T["pt", b, a] = psum.tile([P, NT, P], F32, tag="pt", bufs=2, name="pt")
+            T["pt", b, a] = psum.tile([P, NT, P], F32, tag="pt", bufs=3, name="pt")
             for t in range(NT):
                 nc.tensor.transpose(T["pt", b, a][:, t, :], T["ph", b][:, a, t * P:(t + 1) * P], ident[:])
 
@@ -170,7 +185,7 @@ def tile_neuralsort_kernel(tc, values, scores, out_0, out_1, out_2):
             if a == 0:
                 T["gr", b] = work.tile([P, NT, P, NT], BF16, tag="gr", bufs=2, name="gr", align_bytes=64)
             src = T["pt", b, a][:].rearrange("q t p -> q p t")
-            if a == 0 or (a == 1 and b % 2 == 0):
+            if a == 0:
                 nc.scalar.copy(out=T["gr", b][:, a], in_=src)
             else:
                 nc.vector.tensor_copy(out=T["gr", b][:, a], in_=src)
@@ -203,11 +218,10 @@ def tile_neuralsort_kernel(tc, values, scores, out_0, out_1, out_2):
             nc.sync.dma_start(out=out_0[b].rearrange("(p a) z -> p (a z)", a=NT),
                               in_=osb[:].rearrange("p a z -> p (a z)"))
 
-        eb_pe(0)
+        eb_s(0)
         for k in range(B + 6):
             quant_v(k - 5)
             recip_v(k - 3)
-            eb_pe(k + 1)
             if k < 4:
                 in_regroup(k)
             for x in range(NT):
@@ -216,6 +230,8 @@ def tile_neuralsort_kernel(tc, values, scores, out_0, out_1, out_2):
                     rawt_g(k, 2 * x)
                     p1_s(k, 2 * x + 1)
                     rawt_g(k, 2 * x + 1)
+                if x == 2:
+                    eb_s(k + 1)
                 rp_pe(k - 1, x)
                 evac_v(k - 1, x)
                 exp_s(k - 2, x)

@@ -17,6 +17,27 @@ P = 128
 NT = DIM // P
 FLOPS = 2 * B * DIM * DIM * Z
 
+SLOT = {
+    "eb": (-3.8,),
+    "p1": (-3.5, -2.2, -1.3, -0.5),
+    "rawt": (-2.8, -1.0, -0.8, -0.1),
+    "rp": (3.1, 3.4, 4.9, 5.1),
+    "evac": (4.6, 5.7, 6.3, 6.4),
+    "rawst": (8.4,),
+    "neg": (8.4,),
+    "exp": (9.3, 9.8, 9.0, 9.5),
+    "recip": (12.7,),
+    "p5": (13.3, 13.2, 13.8, 15.0),
+    "phst": (15.6,),
+    "pt": (14.6, 15.2, 16.3, 18.2),
+    "pte": (15.3, 16.7, 18.0, 18.7),
+    "q": (19.0,),
+    "mx": (20.8,),
+    "oe": (22.1,),
+    "inr": (2.5, 6.5, 10.5, 14.5),
+    "inq": (4.5, 8.5, 12.5, 16.5),
+}
+
 
 def tile_neuralsort_kernel(tc, values, scores, out_0, out_1, out_2):
     nc = tc.nc
@@ -45,11 +66,11 @@ def tile_neuralsort_kernel(tc, values, scores, out_0, out_1, out_2):
             nc.sync.dma_start(out=in_raw[:, 4 * g:4 * g + 4], in_=vview[:, 4 * g:4 * g + 4])
 
         sb_load(0, 2)
-        sb_load(2, 8)
         in_load(0)
-        sb_load(8, 16)
+        sb_load(2, 8)
         in_load(1)
         in_load(2)
+        sb_load(8, 16)
         in_load(3)
 
         ident = const.tile([P, P], F32, name="ident")
@@ -71,11 +92,18 @@ def tile_neuralsort_kernel(tc, values, scores, out_0, out_1, out_2):
         icodes = const.tile([P, B, Z], U32, name="icodes", align_bytes=64)
         iscales = const.tile([P, B, Z], U8, name="iscales", align_bytes=64)
 
-        def in_regroup(g):
+        T = {}
+
+        def get(kind, b, make):
+            if (kind, b) not in T:
+                T[kind, b] = make()
+            return T[kind, b]
+
+        def inr(g, a):
             bs = slice(4 * g, 4 * g + 4)
             nc.vector.tensor_copy(out=igr[:, bs], in_=in_raw[:, bs].rearrange("p b t z -> p b z t"))
 
-        def in_quant(g):
+        def inq(g, a):
             bs = slice(4 * g, 4 * g + 4)
             nc.vector.quantize_mx(
                 out=icodes[:, bs].rearrange("p b z -> p (b z)").bitcast(FP8X4),
@@ -83,166 +111,109 @@ def tile_neuralsort_kernel(tc, values, scores, out_0, out_1, out_2):
                 in_=igr[:, bs].rearrange("p b z t -> p (b z t)"),
             )
 
-        T = {}
+        def eb(b, a):
+            t = get("eb", b, lambda: work.tile([P, DIM], F32, tag="eb", bufs=2, name="eb"))
+            nc.scalar.activation(out=t[:], in_=sb[:, b * DIM:(b + 1) * DIM], func=ACT.Exp)
 
-        def ok(b):
-            return 0 <= b < B
-
-        def eb_s(b):
-            if not ok(b):
-                return
-            T["eb", b] = work.tile([P, DIM], F32, tag="eb", bufs=2, name="eb")
-            nc.scalar.activation(out=T["eb", b][:], in_=sb[:, b * DIM:(b + 1) * DIM], func=ACT.Exp)
-
-        def p1_s(b, t):
-            if not ok(b):
-                return
+        def p1(b, t):
             c = b * NT + t
             junk = work.tile([P, DIM], BF16, tag="junk", name="junk")
             nc.scalar.activation(out=junk[:], in_=T["eb", b][:], func=ACT.Abs, bias=e_col[:, c:c + 1],
                                  scale=-1.0, accum_out=r_col[:, c:c + 1])
 
-        def rawt_g(b, t):
-            if not ok(b):
-                return
-            if t == 0:
-                T["nrt", b] = work.tile([P, NT, DIM], F32, tag="nrt", bufs=3, name="nrt")
+        def rawt(b, t):
+            nrt = get("nrt", b, lambda: work.tile([P, NT, DIM], F32, tag="nrt", bufs=3, name="nrt"))
             c = b * NT + t
-            nc.gpsimd.tensor_scalar(out=T["nrt", b][:, t, :], in0=ns[:], scalar1=e_col[:, c:c + 1],
+            nc.gpsimd.tensor_scalar(out=nrt[:, t, :], in0=ns[:], scalar1=e_col[:, c:c + 1],
                                     scalar2=r_col[:, c:c + 1], op0=ALU.mult, op1=ALU.add)
 
-        def rp_pe(b, a):
-            if not ok(b):
-                return
+        def rp(b, a):
             T["rp", b, a] = psum.tile([P, DIM], F32, tag="rp", bufs=4, name="rp")
             for t in range(NT):
                 nc.tensor.transpose(T["rp", b, a][:, t * P:(t + 1) * P], T["nrt", b][:, t, a * P:(a + 1) * P], ident[:])
 
-        def evac_v(b, a):
-            if not ok(b):
-                return
-            if a == 0:
-                T["raw", b] = work.tile([P, NT, DIM], F32, tag="raw", bufs=3, name="raw_sb")
-                T["mx", b] = small.tile([P, NT], F32, tag="mx", name="mx")
-            nc.vector.tensor_scalar(out=T["raw", b][:, a, :], in0=T["rp", b, a][:], scalar1=-1.0, scalar2=None,
-                                    op0=ALU.mult, op1=ALU.max, accum_out=T["mx", b][:, a:a + 1])
+        def evac(b, a):
+            raw = get("raw", b, lambda: work.tile([P, NT, DIM], F32, tag="raw", bufs=3, name="raw_sb"))
+            mx = get("mx", b, lambda: small.tile([P, NT], F32, tag="mx", name="mx"))
+            nc.vector.tensor_scalar(out=raw[:, a, :], in0=T["rp", b, a][:], scalar1=-1.0, scalar2=None,
+                                    op0=ALU.mult, op1=ALU.max, accum_out=mx[:, a:a + 1])
 
-        def raw_store(b):
-            if not ok(b):
-                return
+        def rawst(b, a):
             nc.sync.dma_start(out=out_2[b].rearrange("(p a) i -> p (a i)", a=NT),
                               in_=T["raw", b][:].rearrange("p a i -> p (a i)"))
 
-        def neg_v(b):
-            if not ok(b):
-                return
+        def neg(b, a):
             T["nmx", b] = small.tile([P, NT], F32, tag="nmx", name="nmx")
             nc.vector.tensor_scalar_mul(out=T["nmx", b][:], in0=T["mx", b][:], scalar1=-1.0)
 
-        def exp_s(b, a):
-            if not ok(b):
-                return
-            if a == 0:
-                T["ex", b] = work.tile([P, NT, DIM], F32, tag="ex", bufs=3, name="ex")
-                T["sm", b] = small.tile([P, NT], F32, tag="sm", name="sm")
-            nc.scalar.activation(out=T["ex", b][:, a, :], in_=T["raw", b][:, a, :], func=ACT.Exp,
-                                 bias=T["nmx", b][:, a:a + 1], scale=1.0, accum_out=T["sm", b][:, a:a + 1])
+        def exp(b, a):
+            ex = get("ex", b, lambda: work.tile([P, NT, DIM], F32, tag="ex", bufs=3, name="ex"))
+            sm = get("sm", b, lambda: small.tile([P, NT], F32, tag="sm", name="sm"))
+            nc.scalar.activation(out=ex[:, a, :], in_=T["raw", b][:, a, :], func=ACT.Exp,
+                                 bias=T["nmx", b][:, a:a + 1], scale=1.0, accum_out=sm[:, a:a + 1])
 
-        def recip_v(b):
-            if not ok(b):
-                return
+        def recip(b, a):
             T["rinv", b] = small.tile([P, NT], F32, tag="rinv", name="rinv")
             nc.vector.reciprocal(out=T["rinv", b][:], in_=T["sm", b][:])
 
         def p5(b, a):
-            if not ok(b):
-                return
-            if a == 0:
-                T["ph", b] = work.tile([P, NT, DIM], F32, tag="ph", bufs=3, name="ph")
+            ph = get("ph", b, lambda: work.tile([P, NT, DIM], F32, tag="ph", bufs=3, name="ph"))
             if a != 0:
-                nc.gpsimd.tensor_scalar(out=T["ph", b][:, a, :], in0=T["ex", b][:, a, :],
+                nc.gpsimd.tensor_scalar(out=ph[:, a, :], in0=T["ex", b][:, a, :],
                                         scalar1=T["rinv", b][:, a:a + 1], scalar2=0.0, op0=ALU.mult, op1=ALU.add)
             else:
-                nc.vector.tensor_scalar_mul(out=T["ph", b][:, a, :], in0=T["ex", b][:, a, :],
+                nc.vector.tensor_scalar_mul(out=ph[:, a, :], in0=T["ex", b][:, a, :],
                                             scalar1=T["rinv", b][:, a:a + 1])
 
-        def ph_store(b):
-            if not ok(b):
-                return
+        def phst(b, a):
             nc.sync.dma_start(out=out_1[b].rearrange("(p a) i -> p (a i)", a=NT),
                               in_=T["ph", b][:].rearrange("p a i -> p (a i)"))
 
-        def pt_pe(b, a):
-            if not ok(b):
-                return
+        def pt(b, a):
             T["pt", b, a] = psum.tile([P, NT, P], F32, tag="pt", bufs=3, name="pt")
             for t in range(NT):
                 nc.tensor.transpose(T["pt", b, a][:, t, :], T["ph", b][:, a, t * P:(t + 1) * P], ident[:])
 
-        def pt_evac(b, a):
-            if not ok(b):
-                return
-            if a == 0:
-                T["gr", b] = work.tile([P, NT, P, NT], BF16, tag="gr", bufs=2, name="gr", align_bytes=64)
+        def pte(b, a):
+            gr = get("gr", b, lambda: work.tile([P, NT, P, NT], BF16, tag="gr", bufs=2, name="gr", align_bytes=64))
             src = T["pt", b, a][:].rearrange("q t p -> q p t")
             if a == 0:
-                nc.scalar.copy(out=T["gr", b][:, a], in_=src)
+                nc.scalar.copy(out=gr[:, a], in_=src)
             else:
-                nc.vector.tensor_copy(out=T["gr", b][:, a], in_=src)
+                nc.vector.tensor_copy(out=gr[:, a], in_=src)
 
-        def quant_v(b):
-            if not ok(b):
-                return
+        def q(b, a):
             T["pc", b] = work.tile([P, DIM], U32, tag="pcodes", name="pcodes", align_bytes=64)
             T["ps", b] = work.tile([P, DIM], U8, tag="pscales", name="pscales", align_bytes=64)
             nc.vector.quantize_mx(out=T["pc", b][:].bitcast(FP8X4), scales=T["ps", b][:],
                                   in_=T["gr", b][:].rearrange("q a p t -> q (a p t)"))
 
-        def mx_pe(b):
-            if not ok(b):
-                return
+        def mx(b, a):
             T["op", b] = psum.tile([P, NT, Z], F32, tag="op", bufs=1, name="op")
-            for a in range(NT):
-                nc.tensor.matmul_mx(out=T["op", b][:, a, :],
-                                    lhsT=T["pc", b][:, a * P:(a + 1) * P].bitcast(FP8X4),
-                                    lhsT_scale=T["ps", b][:, a * P:(a + 1) * P],
+            for u in range(NT):
+                nc.tensor.matmul_mx(out=T["op", b][:, u, :],
+                                    lhsT=T["pc", b][:, u * P:(u + 1) * P].bitcast(FP8X4),
+                                    lhsT_scale=T["ps", b][:, u * P:(u + 1) * P],
                                     rhs=icodes[:, b, :].bitcast(FP8X4),
                                     rhs_scale=iscales[:, b, :],
                                     start=True, stop=True)
 
-        def o_evac(b):
-            if not ok(b):
-                return
+        def oe(b, a):
             osb = work.tile([P, NT, Z], F32, tag="osb", bufs=3, name="osb")
             nc.vector.tensor_copy(out=osb[:], in_=T["op", b][:])
             nc.sync.dma_start(out=out_0[b].rearrange("(p a) z -> p (a z)", a=NT),
                               in_=osb[:].rearrange("p a z -> p (a z)"))
 
-        eb_s(0)
-        for k in range(B + 6):
-            quant_v(k - 5)
-            recip_v(k - 3)
-            if k < 4:
-                in_regroup(k)
-            for x in range(NT):
-                if x < 2:
-                    p1_s(k, 2 * x)
-                    rawt_g(k, 2 * x)
-                    p1_s(k, 2 * x + 1)
-                    rawt_g(k, 2 * x + 1)
-                if x == 2:
-                    eb_s(k + 1)
-                rp_pe(k - 1, x)
-                evac_v(k - 1, x)
-                exp_s(k - 2, x)
-                p5(k - 3, x)
-                pt_pe(k - 4, x)
-                pt_evac(k - 4, x)
-                if x == 1:
-                    mx_pe(k - 5)
-            raw_store(k - 1)
-            ph_store(k - 3)
-            neg_v(k - 1)
-            o_evac(k - 5)
-            if k < 4:
-                in_quant(k)
+        per_batch = (("eb", eb), ("p1", p1), ("rawt", rawt), ("rp", rp), ("evac", evac), ("exp", exp), ("p5", p5),
+                     ("pt", pt), ("pte", pte), ("rawst", rawst), ("neg", neg), ("recip", recip), ("phst", phst),
+                     ("q", q), ("mx", mx), ("oe", oe))
+        steps = []
+        for b in range(B):
+            for name, fn in per_batch:
+                for a, off in enumerate(SLOT[name]):
+                    steps.append((NT * b + off, fn, b, a))
+        for name, fn in (("inr", inr), ("inq", inq)):
+            for g, off in enumerate(SLOT[name]):
+                steps.append((off, fn, g, 0))
+        for when, fn, b, a in sorted(steps, key=lambda s: s[0]):
+            fn(b, a)

@@ -17,27 +17,6 @@ P = 128
 NT = DIM // P
 FLOPS = 2 * B * DIM * DIM * Z
 
-SLOT = {
-    "eb": (-3.8,),
-    "p1": (-3.5, -2.2, -1.3, -0.5),
-    "rawt": (-2.8, -1.0, -0.8, -0.1),
-    "rp": (3.1, 3.4, 4.9, 5.1),
-    "evac": (4.6, 5.7, 6.3, 6.4),
-    "rawst": (8.4,),
-    "neg": (8.4,),
-    "exp": (9.3, 9.8, 9.0, 9.5),
-    "recip": (12.7,),
-    "p5": (13.3, 13.2, 13.8, 15.0),
-    "phst": (15.6,),
-    "pt": (14.6, 15.2, 16.3, 18.2),
-    "pte": (15.3, 16.7, 18.0, 18.7),
-    "q": (19.0,),
-    "mx": (20.8,),
-    "oe": (22.1,),
-    "inr": (2.5, 6.5, 10.5, 14.5),
-    "inq": (4.5, 8.5, 12.5, 16.5),
-}
-
 
 def tile_neuralsort_kernel(tc, values, scores, out_0, out_1, out_2):
     nc = tc.nc
@@ -66,11 +45,11 @@ def tile_neuralsort_kernel(tc, values, scores, out_0, out_1, out_2):
             nc.sync.dma_start(out=in_raw[:, 4 * g:4 * g + 4], in_=vview[:, 4 * g:4 * g + 4])
 
         sb_load(0, 2)
-        in_load(0)
         sb_load(2, 8)
+        in_load(0)
+        sb_load(8, 16)
         in_load(1)
         in_load(2)
-        sb_load(8, 16)
         in_load(3)
 
         ident = const.tile([P, P], F32, name="ident")
@@ -92,18 +71,11 @@ def tile_neuralsort_kernel(tc, values, scores, out_0, out_1, out_2):
         icodes = const.tile([P, B, Z], U32, name="icodes", align_bytes=64)
         iscales = const.tile([P, B, Z], U8, name="iscales", align_bytes=64)
 
-        T = {}
-
-        def get(kind, b, make):
-            if (kind, b) not in T:
-                T[kind, b] = make()
-            return T[kind, b]
-
-        def inr(g, a):
+        def in_regroup(g):
             bs = slice(4 * g, 4 * g + 4)
             nc.vector.tensor_copy(out=igr[:, bs], in_=in_raw[:, bs].rearrange("p b t z -> p b z t"))
 
-        def inq(g, a):
+        def in_quant(g):
             bs = slice(4 * g, 4 * g + 4)
             nc.vector.quantize_mx(
                 out=icodes[:, bs].rearrange("p b z -> p (b z)").bitcast(FP8X4),
@@ -111,109 +83,166 @@ def tile_neuralsort_kernel(tc, values, scores, out_0, out_1, out_2):
                 in_=igr[:, bs].rearrange("p b z t -> p (b z t)"),
             )
 
-        def eb(b, a):
-            t = get("eb", b, lambda: work.tile([P, DIM], F32, tag="eb", bufs=2, name="eb"))
-            nc.scalar.activation(out=t[:], in_=sb[:, b * DIM:(b + 1) * DIM], func=ACT.Exp)
+        T = {}
 
-        def p1(b, t):
+        def ok(b):
+            return 0 <= b < B
+
+        def eb_s(b):
+            if not ok(b):
+                return
+            T["eb", b] = work.tile([P, DIM], F32, tag="eb", bufs=2, name="eb")
+            nc.scalar.activation(out=T["eb", b][:], in_=sb[:, b * DIM:(b + 1) * DIM], func=ACT.Exp)
+
+        def p1_s(b, t):
+            if not ok(b):
+                return
             c = b * NT + t
             junk = work.tile([P, DIM], BF16, tag="junk", name="junk")
             nc.scalar.activation(out=junk[:], in_=T["eb", b][:], func=ACT.Abs, bias=e_col[:, c:c + 1],
                                  scale=-1.0, accum_out=r_col[:, c:c + 1])
 
-        def rawt(b, t):
-            nrt = get("nrt", b, lambda: work.tile([P, NT, DIM], F32, tag="nrt", bufs=3, name="nrt"))
+        def rawt_g(b, t):
+            if not ok(b):
+                return
+            if t == 0:
+                T["nrt", b] = work.tile([P, NT, DIM], F32, tag="nrt", bufs=3, name="nrt")
             c = b * NT + t
-            nc.gpsimd.tensor_scalar(out=nrt[:, t, :], in0=ns[:], scalar1=e_col[:, c:c + 1],
+            nc.gpsimd.tensor_scalar(out=T["nrt", b][:, t, :], in0=ns[:], scalar1=e_col[:, c:c + 1],
                                     scalar2=r_col[:, c:c + 1], op0=ALU.mult, op1=ALU.add)
 
-        def rp(b, a):
+        def rp_pe(b, a):
+            if not ok(b):
+                return
             T["rp", b, a] = psum.tile([P, DIM], F32, tag="rp", bufs=4, name="rp")
             for t in range(NT):
                 nc.tensor.transpose(T["rp", b, a][:, t * P:(t + 1) * P], T["nrt", b][:, t, a * P:(a + 1) * P], ident[:])
 
-        def evac(b, a):
-            raw = get("raw", b, lambda: work.tile([P, NT, DIM], F32, tag="raw", bufs=3, name="raw_sb"))
-            mx = get("mx", b, lambda: small.tile([P, NT], F32, tag="mx", name="mx"))
-            nc.vector.tensor_scalar(out=raw[:, a, :], in0=T["rp", b, a][:], scalar1=-1.0, scalar2=None,
-                                    op0=ALU.mult, op1=ALU.max, accum_out=mx[:, a:a + 1])
+        def evac_v(b, a):
+            if not ok(b):
+                return
+            if a == 0:
+                T["raw", b] = work.tile([P, NT, DIM], F32, tag="raw", bufs=3, name="raw_sb")
+                T["mx", b] = small.tile([P, NT], F32, tag="mx", name="mx")
+            nc.vector.tensor_scalar(out=T["raw", b][:, a, :], in0=T["rp", b, a][:], scalar1=-1.0, scalar2=None,
+                                    op0=ALU.mult, op1=ALU.max, accum_out=T["mx", b][:, a:a + 1])
 
-        def rawst(b, a):
+        def raw_store(b):
+            if not ok(b):
+                return
             nc.sync.dma_start(out=out_2[b].rearrange("(p a) i -> p (a i)", a=NT),
                               in_=T["raw", b][:].rearrange("p a i -> p (a i)"))
 
-        def neg(b, a):
+        def neg_v(b):
+            if not ok(b):
+                return
             T["nmx", b] = small.tile([P, NT], F32, tag="nmx", name="nmx")
             nc.vector.tensor_scalar_mul(out=T["nmx", b][:], in0=T["mx", b][:], scalar1=-1.0)
 
-        def exp(b, a):
-            ex = get("ex", b, lambda: work.tile([P, NT, DIM], F32, tag="ex", bufs=3, name="ex"))
-            sm = get("sm", b, lambda: small.tile([P, NT], F32, tag="sm", name="sm"))
-            nc.scalar.activation(out=ex[:, a, :], in_=T["raw", b][:, a, :], func=ACT.Exp,
-                                 bias=T["nmx", b][:, a:a + 1], scale=1.0, accum_out=sm[:, a:a + 1])
+        def exp_s(b, a):
+            if not ok(b):
+                return
+            if a == 0:
+                T["ex", b] = work.tile([P, NT, DIM], F32, tag="ex", bufs=3, name="ex")
+                T["sm", b] = small.tile([P, NT], F32, tag="sm", name="sm")
+            nc.scalar.activation(out=T["ex", b][:, a, :], in_=T["raw", b][:, a, :], func=ACT.Exp,
+                                 bias=T["nmx", b][:, a:a + 1], scale=1.0, accum_out=T["sm", b][:, a:a + 1])
 
-        def recip(b, a):
+        def recip_v(b):
+            if not ok(b):
+                return
             T["rinv", b] = small.tile([P, NT], F32, tag="rinv", name="rinv")
             nc.vector.reciprocal(out=T["rinv", b][:], in_=T["sm", b][:])
 
         def p5(b, a):
-            ph = get("ph", b, lambda: work.tile([P, NT, DIM], F32, tag="ph", bufs=3, name="ph"))
-            if a != 0:
-                nc.gpsimd.tensor_scalar(out=ph[:, a, :], in0=T["ex", b][:, a, :],
+            if not ok(b):
+                return
+            if a == 0:
+                T["ph", b] = work.tile([P, NT, DIM], F32, tag="ph", bufs=3, name="ph")
+            if a % 2 == 1:
+                nc.gpsimd.tensor_scalar(out=T["ph", b][:, a, :], in0=T["ex", b][:, a, :],
                                         scalar1=T["rinv", b][:, a:a + 1], scalar2=0.0, op0=ALU.mult, op1=ALU.add)
             else:
-                nc.vector.tensor_scalar_mul(out=ph[:, a, :], in0=T["ex", b][:, a, :],
+                nc.vector.tensor_scalar_mul(out=T["ph", b][:, a, :], in0=T["ex", b][:, a, :],
                                             scalar1=T["rinv", b][:, a:a + 1])
 
-        def phst(b, a):
+        def ph_store(b):
+            if not ok(b):
+                return
             nc.sync.dma_start(out=out_1[b].rearrange("(p a) i -> p (a i)", a=NT),
                               in_=T["ph", b][:].rearrange("p a i -> p (a i)"))
 
-        def pt(b, a):
+        def pt_pe(b, a):
+            if not ok(b):
+                return
             T["pt", b, a] = psum.tile([P, NT, P], F32, tag="pt", bufs=3, name="pt")
             for t in range(NT):
                 nc.tensor.transpose(T["pt", b, a][:, t, :], T["ph", b][:, a, t * P:(t + 1) * P], ident[:])
 
-        def pte(b, a):
-            gr = get("gr", b, lambda: work.tile([P, NT, P, NT], BF16, tag="gr", bufs=2, name="gr", align_bytes=64))
+        def pt_evac(b, a):
+            if not ok(b):
+                return
+            if a == 0:
+                T["gr", b] = work.tile([P, NT, P, NT], BF16, tag="gr", bufs=2, name="gr", align_bytes=64)
             src = T["pt", b, a][:].rearrange("q t p -> q p t")
             if a == 0:
-                nc.scalar.copy(out=gr[:, a], in_=src)
+                nc.scalar.copy(out=T["gr", b][:, a], in_=src)
             else:
-                nc.vector.tensor_copy(out=gr[:, a], in_=src)
+                nc.vector.tensor_copy(out=T["gr", b][:, a], in_=src)
 
-        def q(b, a):
+        def quant_v(b):
+            if not ok(b):
+                return
             T["pc", b] = work.tile([P, DIM], U32, tag="pcodes", name="pcodes", align_bytes=64)
             T["ps", b] = work.tile([P, DIM], U8, tag="pscales", name="pscales", align_bytes=64)
             nc.vector.quantize_mx(out=T["pc", b][:].bitcast(FP8X4), scales=T["ps", b][:],
                                   in_=T["gr", b][:].rearrange("q a p t -> q (a p t)"))
 
-        def mx(b, a):
+        def mx_pe(b):
+            if not ok(b):
+                return
             T["op", b] = psum.tile([P, NT, Z], F32, tag="op", bufs=1, name="op")
-            for u in range(NT):
-                nc.tensor.matmul_mx(out=T["op", b][:, u, :],
-                                    lhsT=T["pc", b][:, u * P:(u + 1) * P].bitcast(FP8X4),
-                                    lhsT_scale=T["ps", b][:, u * P:(u + 1) * P],
+            for a in range(NT):
+                nc.tensor.matmul_mx(out=T["op", b][:, a, :],
+                                    lhsT=T["pc", b][:, a * P:(a + 1) * P].bitcast(FP8X4),
+                                    lhsT_scale=T["ps", b][:, a * P:(a + 1) * P],
                                     rhs=icodes[:, b, :].bitcast(FP8X4),
                                     rhs_scale=iscales[:, b, :],
                                     start=True, stop=True)
 
-        def oe(b, a):
+        def o_evac(b):
+            if not ok(b):
+                return
             osb = work.tile([P, NT, Z], F32, tag="osb", bufs=3, name="osb")
             nc.vector.tensor_copy(out=osb[:], in_=T["op", b][:])
             nc.sync.dma_start(out=out_0[b].rearrange("(p a) z -> p (a z)", a=NT),
                               in_=osb[:].rearrange("p a z -> p (a z)"))
 
-        per_batch = (("eb", eb), ("p1", p1), ("rawt", rawt), ("rp", rp), ("evac", evac), ("exp", exp), ("p5", p5),
-                     ("pt", pt), ("pte", pte), ("rawst", rawst), ("neg", neg), ("recip", recip), ("phst", phst),
-                     ("q", q), ("mx", mx), ("oe", oe))
-        steps = []
-        for b in range(B):
-            for name, fn in per_batch:
-                for a, off in enumerate(SLOT[name]):
-                    steps.append((NT * b + off, fn, b, a))
-        for name, fn in (("inr", inr), ("inq", inq)):
-            for g, off in enumerate(SLOT[name]):
-                steps.append((off, fn, g, 0))
-        for when, fn, b, a in sorted(steps, key=lambda s: s[0]):
-            fn(b, a)
+        eb_s(0)
+        for k in range(B + 6):
+            quant_v(k - 5)
+            recip_v(k - 3)
+            if k < 4:
+                in_regroup(k)
+            for x in range(NT):
+                if x < 2:
+                    p1_s(k, 2 * x)
+                    rawt_g(k, 2 * x)
+                    p1_s(k, 2 * x + 1)
+                    rawt_g(k, 2 * x + 1)
+                if x == 2:
+                    eb_s(k + 1)
+                rp_pe(k - 1, x)
+                evac_v(k - 1, x)
+                exp_s(k - 2, x)
+                p5(k - 3, x)
+                pt_pe(k - 4, x)
+                pt_evac(k - 4, x)
+                if x == 1:
+                    mx_pe(k - 5)
+            raw_store(k - 1)
+            ph_store(k - 3)
+            neg_v(k - 1)
+            o_evac(k - 5)
+            if k < 4:
+                in_quant(k)

@@ -159,7 +159,7 @@ def tile_neuralsort_kernel(tc, values, scores, out_0, out_1, out_2):
                 return
             if a == 0:
                 T["ph", b] = work.tile([P, NT, DIM], F32, tag="ph", bufs=3, name="ph")
-            if a % 2 == 1:
+            if a != 0:
                 nc.gpsimd.tensor_scalar(out=T["ph", b][:, a, :], in0=T["ex", b][:, a, :],
                                         scalar1=T["rinv", b][:, a:a + 1], scalar2=0.0, op0=ALU.mult, op1=ALU.add)
             else:
@@ -214,7 +214,7 @@ def tile_neuralsort_kernel(tc, values, scores, out_0, out_1, out_2):
             if not ok(b):
                 return
             osb = work.tile([P, NT, Z], F32, tag="osb", bufs=3, name="osb")
-            nc.vector.tensor_copy(out=osb[:], in_=T["op", b][:])
+            nc.scalar.copy(out=osb[:], in_=T["op", b][:])
             nc.sync.dma_start(out=out_0[b].rearrange("(p a) z -> p (a z)", a=NT),
                               in_=osb[:].rearrange("p a z -> p (a z)"))
 

@@ -57,14 +57,23 @@ def tile_neuralsort_kernel(tc, values, scores, out_0, out_1, out_2):
         ns_int = const.tile([P, NT, P], I32, name="ns_int")
         nc.gpsimd.iota(ns_int[:], pattern=[[2, NT], [8, P]], base=-(DIM - 1), channel_multiplier=0)
         ns = const.tile([P, DIM], F32, name="ns")
-        nc.vector.tensor_copy(out=ns[:], in_=ns_int[:].rearrange("p a q -> p (a q)"))
+        nc.vector.tensor_scalar_mul(out=ns[:], in0=ns_int[:].rearrange("p a q -> p (a q)"), scalar1=0.5)
 
-        e_rows = const.tile([P, P], F32, name="e_rows")
-        nc.scalar.activation(out=e_rows[:], in_=sc[:], func=ACT.Exp)
-        e_ps = psum.tile([P, DIM], F32, tag="pt", bufs=3, name="e_ps")
-        nc.tensor.transpose(e_ps[:, 0:P], e_rows[:], ident[:])
+        s_rows = const.tile([P, P], F32, name="s_rows")
+        nc.vector.tensor_copy(out=s_rows[:], in_=sc[:])
+        s_ps = psum.tile([P, DIM], F32, tag="pt", bufs=3, name="s_ps")
+        nc.tensor.transpose(s_ps[:, 0:P], s_rows[:], ident[:])
+        s_col = const.tile([P, B * NT], F32, name="s_col")
         e_col = const.tile([P, B * NT], F32, name="e_col")
-        nc.vector.tensor_copy(out=e_col[:], in_=e_ps[:, 0:B * NT])
+        nc.scalar.activation(out=e_col[:], in_=s_ps[:, 0:B * NT], func=ACT.Exp)
+        nc.vector.tensor_copy(out=s_col[:], in_=s_ps[:, 0:B * NT])
+        e_terms = const.tile([P, B * NT, 4], BF16, name="e_terms")
+        d1 = const.tile([P, B * NT], F32, name="d1")
+        nc.vector.memset(e_terms[:, :, 3], 1.0)
+        nc.vector.tensor_copy(out=e_terms[:, :, 0], in_=e_col[:])
+        nc.vector.tensor_sub(out=d1[:], in0=e_col[:], in1=e_terms[:, :, 0])
+        nc.vector.tensor_copy(out=e_terms[:, :, 1], in_=d1[:])
+        nc.vector.tensor_sub(out=e_terms[:, :, 2], in0=d1[:], in1=e_terms[:, :, 1])
         r_col = const.tile([P, B * NT], F32, name="r_col")
 
         igr = const.tile([P, B, Z, NT], BF16, name="igr", align_bytes=64)
@@ -88,19 +97,33 @@ def tile_neuralsort_kernel(tc, values, scores, out_0, out_1, out_2):
         def ok(b):
             return 0 <= b < B
 
-        def eb_s(b):
+        def cmp_v(b):
             if not ok(b):
                 return
-            T["eb", b] = work.tile([P, DIM], F32, tag="eb", bufs=2, name="eb")
-            nc.scalar.activation(out=T["eb", b][:], in_=sb[:, b * DIM:(b + 1) * DIM], func=ACT.Exp)
+            for t in range(NT):
+                c = b * NT + t
+                T["q", b, t] = work.tile([P, DIM], BF16, tag="q%d" % t, bufs=2, name="q")
+                nc.vector.tensor_scalar(out=T["q", b, t][:], in0=sb[:, b * DIM:(b + 1) * DIM], scalar1=s_col[:, c:c + 1],
+                                        scalar2=0.5, op0=ALU.is_le, op1=ALU.subtract)
 
-        def p1_s(b, t):
+        def row_pe(b):
             if not ok(b):
                 return
-            c = b * NT + t
-            junk = work.tile([P, DIM], BF16, tag="junk", name="junk")
-            nc.scalar.activation(out=junk[:], in_=T["eb", b][:], func=ACT.Abs, bias=e_col[:, c:c + 1],
-                                 scale=-1.0, accum_out=r_col[:, c:c + 1])
+            T["rs", b] = psum.tile([P, NT, 4], F32, tag="rs", bufs=1, name="rs")
+            for a in range(NT):
+                for t in range(NT):
+                    nc.tensor.matmul(T["rs", b][:, a, :], lhsT=T["q", b, t][:, a * P:(a + 1) * P],
+                                     rhs=e_terms[:, b * NT + t, :], start=(t == 0), stop=(t == NT - 1))
+
+        def row_v(b):
+            if not ok(b):
+                return
+            cs = slice(b * NT, (b + 1) * NT)
+            cnt = small.tile([P, NT], F32, tag="cnt", name="cnt")
+            tot = small.tile([P, NT], F32, tag="tot", name="tot")
+            nc.vector.tensor_tensor(out=cnt[:], in0=T["rs", b][:, :, 3], in1=e_col[:, cs], op=ALU.mult)
+            nc.vector.tensor_reduce(out=tot[:], in_=T["rs", b][:, :, 0:3], axis=mybir.AxisListType.X, op=ALU.add)
+            nc.vector.tensor_sub(out=r_col[:, cs], in0=tot[:], in1=cnt[:])
 
         def rawt_g(b, t):
             if not ok(b):
@@ -114,7 +137,7 @@ def tile_neuralsort_kernel(tc, values, scores, out_0, out_1, out_2):
         def rp_pe(b, a):
             if not ok(b):
                 return
-            T["rp", b, a] = psum.tile([P, DIM], F32, tag="rp", bufs=4, name="rp")
+            T["rp", b, a] = psum.tile([P, DIM], F32, tag="rp", bufs=3, name="rp")
             for t in range(NT):
                 nc.tensor.transpose(T["rp", b, a][:, t * P:(t + 1) * P], T["nrt", b][:, t, a * P:(a + 1) * P], ident[:])
 
@@ -124,7 +147,7 @@ def tile_neuralsort_kernel(tc, values, scores, out_0, out_1, out_2):
             if a == 0:
                 T["raw", b] = work.tile([P, NT, DIM], F32, tag="raw", bufs=3, name="raw_sb")
                 T["mx", b] = small.tile([P, NT], F32, tag="mx", name="mx")
-            nc.vector.tensor_scalar(out=T["raw", b][:, a, :], in0=T["rp", b, a][:], scalar1=-1.0, scalar2=None,
+            nc.vector.tensor_scalar(out=T["raw", b][:, a, :], in0=T["rp", b, a][:], scalar1=-2.0, scalar2=None,
                                     op0=ALU.mult, op1=ALU.max, accum_out=T["mx", b][:, a:a + 1])
 
         def raw_store(b):
@@ -185,7 +208,7 @@ def tile_neuralsort_kernel(tc, values, scores, out_0, out_1, out_2):
             if a == 0:
                 T["gr", b] = work.tile([P, NT, P, NT], BF16, tag="gr", bufs=2, name="gr", align_bytes=64)
             src = T["pt", b, a][:].rearrange("q t p -> q p t")
-            if a == 0:
+            if a < 3:
                 nc.scalar.copy(out=T["gr", b][:, a], in_=src)
             else:
                 nc.vector.tensor_copy(out=T["gr", b][:, a], in_=src)
@@ -218,20 +241,18 @@ def tile_neuralsort_kernel(tc, values, scores, out_0, out_1, out_2):
             nc.sync.dma_start(out=out_0[b].rearrange("(p a) z -> p (a z)", a=NT),
                               in_=osb[:].rearrange("p a z -> p (a z)"))
 
-        eb_s(0)
+        cmp_v(0)
+        row_pe(0)
+        row_v(0)
         for k in range(B + 6):
             quant_v(k - 5)
             recip_v(k - 3)
             if k < 4:
                 in_regroup(k)
+            cmp_v(k + 1)
+            row_pe(k + 1)
             for x in range(NT):
-                if x < 2:
-                    p1_s(k, 2 * x)
-                    rawt_g(k, 2 * x)
-                    p1_s(k, 2 * x + 1)
-                    rawt_g(k, 2 * x + 1)
-                if x == 2:
-                    eb_s(k + 1)
+                rawt_g(k, x)
                 rp_pe(k - 1, x)
                 evac_v(k - 1, x)
                 exp_s(k - 2, x)
@@ -239,6 +260,7 @@ def tile_neuralsort_kernel(tc, values, scores, out_0, out_1, out_2):
                 pt_pe(k - 4, x)
                 pt_evac(k - 4, x)
                 if x == 1:
+                    row_v(k + 1)
                     mx_pe(k - 5)
             raw_store(k - 1)
             ph_store(k - 3)

@@ -15,6 +15,8 @@ ACT = mybir.ActivationFunctionType
 B, DIM, Z = 16, 512, 128
 P = 128
 NT = DIM // P
+P5 = "VGVS"
+PT = "SSSV"
 FLOPS = 2 * B * DIM * DIM * Z
 
 
@@ -97,23 +99,22 @@ def tile_neuralsort_kernel(tc, values, scores, out_0, out_1, out_2):
         def ok(b):
             return 0 <= b < B
 
-        def cmp_v(b):
+        def cmp_v(b, t):
             if not ok(b):
                 return
-            for t in range(NT):
-                c = b * NT + t
-                T["q", b, t] = work.tile([P, DIM], BF16, tag="q%d" % t, bufs=2, name="q")
-                nc.vector.tensor_scalar(out=T["q", b, t][:], in0=sb[:, b * DIM:(b + 1) * DIM], scalar1=s_col[:, c:c + 1],
-                                        scalar2=0.5, op0=ALU.is_le, op1=ALU.subtract)
+            c = b * NT + t
+            T["q", b, t] = work.tile([P, DIM], BF16, tag="q%d" % t, bufs=3, name="q")
+            nc.vector.tensor_scalar(out=T["q", b, t][:], in0=sb[:, b * DIM:(b + 1) * DIM], scalar1=s_col[:, c:c + 1],
+                                    scalar2=0.5, op0=ALU.is_le, op1=ALU.subtract)
 
-        def row_pe(b):
+        def row_pe(b, a):
             if not ok(b):
                 return
-            T["rs", b] = psum.tile([P, NT, 4], F32, tag="rs", bufs=1, name="rs")
-            for a in range(NT):
-                for t in range(NT):
-                    nc.tensor.matmul(T["rs", b][:, a, :], lhsT=T["q", b, t][:, a * P:(a + 1) * P],
-                                     rhs=e_terms[:, b * NT + t, :], start=(t == 0), stop=(t == NT - 1))
+            if a == 0:
+                T["rs", b] = psum.tile([P, NT, 4], F32, tag="rs", bufs=1, name="rs")
+            for t in range(NT):
+                nc.tensor.matmul(T["rs", b][:, a, :], lhsT=T["q", b, t][:, a * P:(a + 1) * P],
+                                 rhs=e_terms[:, b * NT + t, :], start=(t == 0), stop=(t == NT - 1))
 
         def row_v(b):
             if not ok(b):
@@ -123,7 +124,7 @@ def tile_neuralsort_kernel(tc, values, scores, out_0, out_1, out_2):
             tot = small.tile([P, NT], F32, tag="tot", name="tot")
             nc.vector.tensor_tensor(out=cnt[:], in0=T["rs", b][:, :, 3], in1=e_col[:, cs], op=ALU.mult)
             nc.vector.tensor_reduce(out=tot[:], in_=T["rs", b][:, :, 0:3], axis=mybir.AxisListType.X, op=ALU.add)
-            nc.vector.tensor_sub(out=r_col[:, cs], in0=tot[:], in1=cnt[:])
+            nc.gpsimd.tensor_sub(out=r_col[:, cs], in0=tot[:], in1=cnt[:])
 
         def rawt_g(b, t):
             if not ok(b):
@@ -156,11 +157,11 @@ def tile_neuralsort_kernel(tc, values, scores, out_0, out_1, out_2):
             nc.sync.dma_start(out=out_2[b].rearrange("(p a) i -> p (a i)", a=NT),
                               in_=T["raw", b][:].rearrange("p a i -> p (a i)"))
 
-        def neg_v(b):
+        def neg_s(b):
             if not ok(b):
                 return
             T["nmx", b] = small.tile([P, NT], F32, tag="nmx", name="nmx")
-            nc.vector.tensor_scalar_mul(out=T["nmx", b][:], in0=T["mx", b][:], scalar1=-1.0)
+            nc.scalar.mul(out=T["nmx", b][:], in_=T["mx", b][:], mul=-1.0)
 
         def exp_s(b, a):
             if not ok(b):
@@ -182,12 +183,13 @@ def tile_neuralsort_kernel(tc, values, scores, out_0, out_1, out_2):
                 return
             if a == 0:
                 T["ph", b] = work.tile([P, NT, DIM], F32, tag="ph", bufs=3, name="ph")
-            if a != 0:
-                nc.gpsimd.tensor_scalar(out=T["ph", b][:, a, :], in0=T["ex", b][:, a, :],
-                                        scalar1=T["rinv", b][:, a:a + 1], scalar2=0.0, op0=ALU.mult, op1=ALU.add)
+            src, dst, rcp = T["ex", b][:, a, :], T["ph", b][:, a, :], T["rinv", b][:, a:a + 1]
+            if P5[a] == "V":
+                nc.vector.tensor_scalar_mul(out=dst, in0=src, scalar1=rcp)
+            elif P5[a] == "S":
+                nc.scalar.activation(out=dst, in_=src, func=ACT.Copy, scale=rcp)
             else:
-                nc.vector.tensor_scalar_mul(out=T["ph", b][:, a, :], in0=T["ex", b][:, a, :],
-                                            scalar1=T["rinv", b][:, a:a + 1])
+                nc.gpsimd.tensor_scalar(out=dst, in0=src, scalar1=rcp, scalar2=0.0, op0=ALU.mult, op1=ALU.add)
 
         def ph_store(b):
             if not ok(b):
@@ -208,7 +210,7 @@ def tile_neuralsort_kernel(tc, values, scores, out_0, out_1, out_2):
             if a == 0:
                 T["gr", b] = work.tile([P, NT, P, NT], BF16, tag="gr", bufs=2, name="gr", align_bytes=64)
             src = T["pt", b, a][:].rearrange("q t p -> q p t")
-            if a < 3:
+            if PT[a] == "S":
                 nc.scalar.copy(out=T["gr", b][:, a], in_=src)
             else:
                 nc.vector.tensor_copy(out=T["gr", b][:, a], in_=src)
@@ -241,30 +243,43 @@ def tile_neuralsort_kernel(tc, values, scores, out_0, out_1, out_2):
             nc.sync.dma_start(out=out_0[b].rearrange("(p a) z -> p (a z)", a=NT),
                               in_=osb[:].rearrange("p a z -> p (a z)"))
 
-        cmp_v(0)
-        row_pe(0)
+        for t in range(NT):
+            cmp_v(0, t)
+        for a in range(NT):
+            row_pe(0, a)
+        for t in range(NT):
+            cmp_v(1, t)
         row_v(0)
         for k in range(B + 6):
-            quant_v(k - 5)
-            recip_v(k - 3)
-            if k < 4:
-                in_regroup(k)
-            cmp_v(k + 1)
-            row_pe(k + 1)
             for x in range(NT):
-                rawt_g(k, x)
+                if x == 0:
+                    recip_v(k - 3)
                 rp_pe(k - 1, x)
+                pt_pe(k - 4, x)
+                rawt_g(k, x)
                 evac_v(k - 1, x)
                 exp_s(k - 2, x)
-                p5(k - 3, x)
-                pt_pe(k - 4, x)
                 pt_evac(k - 4, x)
+                if x == 0:
+                    quant_v(k - 5)
+                    for a in range(NT):
+                        p5(k - 3, a)
+                    for t in range(NT):
+                        cmp_v(k + 2, t)
+                    if k % 4 == 2 and k < B:
+                        in_regroup(k // 4)
+                    if k % 4 == 3 and k < B:
+                        in_quant(k // 4)
+                if x == 0:
+                    row_pe(k + 1, 0)
                 if x == 1:
-                    row_v(k + 1)
+                    row_pe(k + 1, 1)
+                    row_pe(k + 1, 2)
+                if x == 2:
+                    row_pe(k + 1, 3)
                     mx_pe(k - 5)
+                    row_v(k + 1)
+            neg_s(k - 1)
             raw_store(k - 1)
             ph_store(k - 3)
-            neg_v(k - 1)
             o_evac(k - 5)
-            if k < 4:
-                in_quant(k)

@@ -16,7 +16,13 @@ B, DIM, Z = 16, 512, 128
 P = 128
 NT = DIM // P
 P5 = "VGVS"
+IN = "SSVV"
+NRT = {0: "VVSG", 1: "VSGG"}
 PT = "SSSV"
+OTAIL = 15
+TAIL = 13
+PT_TAIL = "VVVS"
+P5_TAIL = "VGVG"
 FLOPS = 2 * B * DIM * DIM * Z
 
 
@@ -46,11 +52,10 @@ def tile_neuralsort_kernel(tc, values, scores, out_0, out_1, out_2):
         def in_load(g):
             nc.sync.dma_start(out=in_raw[:, 4 * g:4 * g + 4], in_=vview[:, 4 * g:4 * g + 4])
 
-        sb_load(0, 2)
-        sb_load(2, 8)
+        sb_load(0, 3)
         in_load(0)
-        sb_load(8, 16)
         in_load(1)
+        sb_load(3, 16)
         in_load(2)
         in_load(3)
 
@@ -84,7 +89,11 @@ def tile_neuralsort_kernel(tc, values, scores, out_0, out_1, out_2):
 
         def in_regroup(g):
             bs = slice(4 * g, 4 * g + 4)
-            nc.vector.tensor_copy(out=igr[:, bs], in_=in_raw[:, bs].rearrange("p b t z -> p b z t"))
+            src = in_raw[:, bs].rearrange("p b t z -> p b z t")
+            if IN[g] == "S":
+                nc.scalar.copy(out=igr[:, bs], in_=src)
+            else:
+                nc.vector.tensor_copy(out=igr[:, bs], in_=src)
 
         def in_quant(g):
             bs = slice(4 * g, 4 * g + 4)
@@ -95,6 +104,12 @@ def tile_neuralsort_kernel(tc, values, scores, out_0, out_1, out_2):
             )
 
         T = {}
+
+        def pt_on(b):
+            return PT if b < TAIL else PT_TAIL
+
+        def p5_on(b):
+            return P5 if b < TAIL else P5_TAIL
 
         def ok(b):
             return 0 <= b < B
@@ -124,7 +139,12 @@ def tile_neuralsort_kernel(tc, values, scores, out_0, out_1, out_2):
             tot = small.tile([P, NT], F32, tag="tot", name="tot")
             nc.vector.tensor_tensor(out=cnt[:], in0=T["rs", b][:, :, 3], in1=e_col[:, cs], op=ALU.mult)
             nc.vector.tensor_reduce(out=tot[:], in_=T["rs", b][:, :, 0:3], axis=mybir.AxisListType.X, op=ALU.add)
-            nc.gpsimd.tensor_sub(out=r_col[:, cs], in0=tot[:], in1=cnt[:])
+            T["cnt", b], T["tot", b] = cnt, tot
+
+        def row_g(b):
+            if not ok(b):
+                return
+            nc.gpsimd.tensor_sub(out=r_col[:, b * NT:(b + 1) * NT], in0=T["tot", b][:], in1=T["cnt", b][:])
 
         def rawt_g(b, t):
             if not ok(b):
@@ -132,8 +152,14 @@ def tile_neuralsort_kernel(tc, values, scores, out_0, out_1, out_2):
             if t == 0:
                 T["nrt", b] = work.tile([P, NT, DIM], F32, tag="nrt", bufs=3, name="nrt")
             c = b * NT + t
-            nc.gpsimd.tensor_scalar(out=T["nrt", b][:, t, :], in0=ns[:], scalar1=e_col[:, c:c + 1],
-                                    scalar2=r_col[:, c:c + 1], op0=ALU.mult, op1=ALU.add)
+            ec, rc, dst = e_col[:, c:c + 1], r_col[:, c:c + 1], T["nrt", b][:, t, :]
+            eng = NRT.get(b, "GGGG")[t]
+            if eng == "S":
+                nc.scalar.activation(out=dst, in_=ns[:], func=ACT.Identity, scale=ec, bias=rc)
+            elif eng == "V":
+                nc.vector.tensor_scalar(out=dst, in0=ns[:], scalar1=ec, scalar2=rc, op0=ALU.mult, op1=ALU.add)
+            else:
+                nc.gpsimd.tensor_scalar(out=dst, in0=ns[:], scalar1=ec, scalar2=rc, op0=ALU.mult, op1=ALU.add)
 
         def rp_pe(b, a):
             if not ok(b):
@@ -151,8 +177,11 @@ def tile_neuralsort_kernel(tc, values, scores, out_0, out_1, out_2):
             nc.vector.tensor_scalar(out=T["raw", b][:, a, :], in0=T["rp", b, a][:], scalar1=-2.0, scalar2=None,
                                     op0=ALU.mult, op1=ALU.max, accum_out=T["mx", b][:, a:a + 1])
 
-        def raw_store(b):
+        def raw_store(b, a=None):
             if not ok(b):
+                return
+            if a is not None:
+                nc.sync.dma_start(out=out_2[b].rearrange("(p a) i -> p a i", a=NT)[:, a, :], in_=T["raw", b][:, a, :])
                 return
             nc.sync.dma_start(out=out_2[b].rearrange("(p a) i -> p (a i)", a=NT),
                               in_=T["raw", b][:].rearrange("p a i -> p (a i)"))
@@ -184,9 +213,10 @@ def tile_neuralsort_kernel(tc, values, scores, out_0, out_1, out_2):
             if a == 0:
                 T["ph", b] = work.tile([P, NT, DIM], F32, tag="ph", bufs=3, name="ph")
             src, dst, rcp = T["ex", b][:, a, :], T["ph", b][:, a, :], T["rinv", b][:, a:a + 1]
-            if P5[a] == "V":
+            eng = p5_on(b)[a]
+            if eng == "V":
                 nc.vector.tensor_scalar_mul(out=dst, in0=src, scalar1=rcp)
-            elif P5[a] == "S":
+            elif eng == "S":
                 nc.scalar.activation(out=dst, in_=src, func=ACT.Copy, scale=rcp)
             else:
                 nc.gpsimd.tensor_scalar(out=dst, in0=src, scalar1=rcp, scalar2=0.0, op0=ALU.mult, op1=ALU.add)
@@ -210,7 +240,7 @@ def tile_neuralsort_kernel(tc, values, scores, out_0, out_1, out_2):
             if a == 0:
                 T["gr", b] = work.tile([P, NT, P, NT], BF16, tag="gr", bufs=2, name="gr", align_bytes=64)
             src = T["pt", b, a][:].rearrange("q t p -> q p t")
-            if PT[a] == "S":
+            if pt_on(b)[a] == "S":
                 nc.scalar.copy(out=T["gr", b][:, a], in_=src)
             else:
                 nc.vector.tensor_copy(out=T["gr", b][:, a], in_=src)
@@ -239,7 +269,10 @@ def tile_neuralsort_kernel(tc, values, scores, out_0, out_1, out_2):
             if not ok(b):
                 return
             osb = work.tile([P, NT, Z], F32, tag="osb", bufs=3, name="osb")
-            nc.scalar.copy(out=osb[:], in_=T["op", b][:])
+            if b < OTAIL:
+                nc.scalar.copy(out=osb[:], in_=T["op", b][:])
+            else:
+                nc.vector.tensor_copy(out=osb[:], in_=T["op", b][:])
             nc.sync.dma_start(out=out_0[b].rearrange("(p a) z -> p (a z)", a=NT),
                               in_=osb[:].rearrange("p a z -> p (a z)"))
 
@@ -250,14 +283,28 @@ def tile_neuralsort_kernel(tc, values, scores, out_0, out_1, out_2):
         for t in range(NT):
             cmp_v(1, t)
         row_v(0)
-        for k in range(B + 6):
+        row_g(0)
+        for t in range(NT):
+            rawt_g(0, t)
+        in_regroup(0)
+        in_regroup(1)
+        for a in range(NT):
+            row_pe(1, a)
+        for t in range(NT):
+            cmp_v(2, t)
+        row_v(1)
+        row_g(1)
+        for k in range(1, B + 6):
             for x in range(NT):
                 if x == 0:
                     recip_v(k - 3)
+                    for t in range(NT):
+                        rawt_g(k, t)
                 rp_pe(k - 1, x)
                 pt_pe(k - 4, x)
-                rawt_g(k, x)
                 evac_v(k - 1, x)
+                if k == 1:
+                    raw_store(0, x)
                 exp_s(k - 2, x)
                 pt_evac(k - 4, x)
                 if x == 0:
@@ -266,20 +313,20 @@ def tile_neuralsort_kernel(tc, values, scores, out_0, out_1, out_2):
                         p5(k - 3, a)
                     for t in range(NT):
                         cmp_v(k + 2, t)
-                    if k % 4 == 2 and k < B:
-                        in_regroup(k // 4)
-                    if k % 4 == 3 and k < B:
-                        in_quant(k // 4)
-                if x == 0:
-                    row_pe(k + 1, 0)
+                    if k in (4, 8):
+                        in_regroup(2 + (k == 8))
+                    if k in (2, 3, 5, 9):
+                        in_quant((2, 3, 5, 9).index(k))
                 if x == 1:
-                    row_pe(k + 1, 1)
-                    row_pe(k + 1, 2)
+                    for a in range(NT):
+                        row_pe(k + 1, a)
                 if x == 2:
-                    row_pe(k + 1, 3)
                     mx_pe(k - 5)
+                if x == 2:
                     row_v(k + 1)
+                    row_g(k + 1)
             neg_s(k - 1)
-            raw_store(k - 1)
+            if k != 1:
+                raw_store(k - 1)
             ph_store(k - 3)
             o_evac(k - 5)

from contextlib import ExitStack

import concourse.mybir as mybir
from concourse.masks import make_identity

F32 = mybir.dt.float32
BF16 = mybir.dt.bfloat16
I32 = mybir.dt.int32
U32 = mybir.dt.uint32
U8 = mybir.dt.uint8
FP8X4 = mybir.dt.float8_e4m3fn_x4
ALU = mybir.AluOpType
ACT = mybir.ActivationFunctionType

B, DIM, Z = 16, 512, 128
P = 128
NT = DIM // P
P5 = "VGVS"
IN = "SSVV"
NRT = {0: "VVSG", 1: "VSGG"}
PT = "SSSV"
OTAIL = 15
TAIL = 13
PT_TAIL = "VVVS"
P5_TAIL = "VGVG"
FLOPS = 2 * B * DIM * DIM * Z


def tile_neuralsort_kernel(tc, values, scores, out_0, out_1, out_2):
    nc = tc.nc
    with ExitStack() as ctx:
        const = ctx.enter_context(tc.tile_pool(name="const", bufs=1))
        work = ctx.enter_context(tc.tile_pool(name="work", bufs=2))
        small = ctx.enter_context(tc.tile_pool(name="small", bufs=4))
        psum = ctx.enter_context(tc.psum_pool(name="psum", bufs=1))
        ctx.enter_context(tc.manual_schedule())

        warm = const.tile([P, 1], F32, name="warm")
        nc.vector.memset(warm[:], 0.0)
        nc.scalar.activation(out=warm[:], in_=warm[:], func=ACT.Exp)
        sc = const.tile([P, P], BF16, name="sc")
        nc.vector.memset(sc[64:128, :], 0.0)
        nc.sync.dma_start(out=sc[0:64, :], in_=scores.rearrange("b (t q) -> (b t) q", q=P))
        sb = const.tile([P, B * DIM], BF16, name="sb")
        sflat = scores.rearrange("b i -> (b i)")
        in_raw = const.tile([P, B, NT, Z], BF16, name="in_raw")
        vview = values.rearrange("b (t q) z -> q b t z", q=P)

        def sb_load(b0, b1):
            nc.sync.dma_start(out=sb[:, b0 * DIM:b1 * DIM], in_=sflat[b0 * DIM:b1 * DIM].partition_broadcast(P))

        def in_load(g):
            nc.sync.dma_start(out=in_raw[:, 4 * g:4 * g + 4], in_=vview[:, 4 * g:4 * g + 4])

        sb_load(0, 3)
        in_load(0)
        in_load(1)
        sb_load(3, 16)
        in_load(2)
        in_load(3)

        ident = const.tile([P, P], F32, name="ident")
        make_identity(nc, ident[:])
        ns_int = const.tile([P, NT, P], I32, name="ns_int")
        nc.gpsimd.iota(ns_int[:], pattern=[[2, NT], [8, P]], base=-(DIM - 1), channel_multiplier=0)
        ns = const.tile([P, DIM], F32, name="ns")
        nc.vector.tensor_scalar_mul(out=ns[:], in0=ns_int[:].rearrange("p a q -> p (a q)"), scalar1=0.5)

        s_rows = const.tile([P, P], F32, name="s_rows")
        nc.vector.tensor_copy(out=s_rows[:], in_=sc[:])
        s_ps = psum.tile([P, DIM], F32, tag="pt", bufs=3, name="s_ps")
        nc.tensor.transpose(s_ps[:, 0:P], s_rows[:], ident[:])
        s_col = const.tile([P, B * NT], F32, name="s_col")
        e_col = const.tile([P, B * NT], F32, name="e_col")
        nc.scalar.activation(out=e_col[:], in_=s_ps[:, 0:B * NT], func=ACT.Exp)
        nc.vector.tensor_copy(out=s_col[:], in_=s_ps[:, 0:B * NT])
        e_terms = const.tile([P, B * NT, 4], BF16, name="e_terms")
        d1 = const.tile([P, B * NT], F32, name="d1")
        nc.vector.memset(e_terms[:, :, 3], 1.0)
        nc.vector.tensor_copy(out=e_terms[:, :, 0], in_=e_col[:])
        nc.vector.tensor_sub(out=d1[:], in0=e_col[:], in1=e_terms[:, :, 0])
        nc.vector.tensor_copy(out=e_terms[:, :, 1], in_=d1[:])
        nc.vector.tensor_sub(out=e_terms[:, :, 2], in0=d1[:], in1=e_terms[:, :, 1])
        r_col = const.tile([P, B * NT], F32, name="r_col")

        igr = const.tile([P, B, Z, NT], BF16, name="igr", align_bytes=64)
        icodes = const.tile([P, B, Z], U32, name="icodes", align_bytes=64)
        iscales = const.tile([P, B, Z], U8, name="iscales", align_bytes=64)

        def in_regroup(g):
            bs = slice(4 * g, 4 * g + 4)
            src = in_raw[:, bs].rearrange("p b t z -> p b z t")
            if IN[g] == "S":
                nc.scalar.copy(out=igr[:, bs], in_=src)
            else:
                nc.vector.tensor_copy(out=igr[:, bs], in_=src)

        def in_quant(g):
            bs = slice(4 * g, 4 * g + 4)
            nc.vector.quantize_mx(
                out=icodes[:, bs].rearrange("p b z -> p (b z)").bitcast(FP8X4),
                scales=iscales[:, bs].rearrange("p b z -> p (b z)"),
                in_=igr[:, bs].rearrange("p b z t -> p (b z t)"),
            )

        T = {}

        def pt_on(b):
            return PT if b < TAIL else PT_TAIL

        def p5_on(b):
            return P5 if b < TAIL else P5_TAIL

        def ok(b):
            return 0 <= b < B

        def cmp_v(b, t):
            if not ok(b):
                return
            c = b * NT + t
            T["q", b, t] = work.tile([P, DIM], BF16, tag="q%d" % t, bufs=3, name="q")
            nc.vector.tensor_scalar(out=T["q", b, t][:], in0=sb[:, b * DIM:(b + 1) * DIM], scalar1=s_col[:, c:c + 1],
                                    scalar2=0.5, op0=ALU.is_le, op1=ALU.subtract)

        def row_pe(b, a):
            if not ok(b):
                return
            if a == 0:
                T["rs", b] = psum.tile([P, NT, 4], F32, tag="rs", bufs=1, name="rs")
            for t in range(NT):
                nc.tensor.matmul(T["rs", b][:, a, :], lhsT=T["q", b, t][:, a * P:(a + 1) * P],
                                 rhs=e_terms[:, b * NT + t, :], start=(t == 0), stop=(t == NT - 1))

        def row_v(b):
            if not ok(b):
                return
            cs = slice(b * NT, (b + 1) * NT)
            cnt = small.tile([P, NT], F32, tag="cnt", name="cnt")
            tot = small.tile([P, NT], F32, tag="tot", name="tot")
            nc.vector.tensor_tensor(out=cnt[:], in0=T["rs", b][:, :, 3], in1=e_col[:, cs], op=ALU.mult)
            nc.vector.tensor_reduce(out=tot[:], in_=T["rs", b][:, :, 0:3], axis=mybir.AxisListType.X, op=ALU.add)
            T["cnt", b], T["tot", b] = cnt, tot

        def row_g(b):
            if not ok(b):
                return
            nc.gpsimd.tensor_sub(out=r_col[:, b * NT:(b + 1) * NT], in0=T["tot", b][:], in1=T["cnt", b][:])

        def rawt_g(b, t):
            if not ok(b):
                return
            if t == 0:
                T["nrt", b] = work.tile([P, NT, DIM], F32, tag="nrt", bufs=3, name="nrt")
            c = b * NT + t
            ec, rc, dst = e_col[:, c:c + 1], r_col[:, c:c + 1], T["nrt", b][:, t, :]
            eng = NRT.get(b, "GGGG")[t]
            if eng == "S":
                nc.scalar.activation(out=dst, in_=ns[:], func=ACT.Identity, scale=ec, bias=rc)
            elif eng == "V":
                nc.vector.tensor_scalar(out=dst, in0=ns[:], scalar1=ec, scalar2=rc, op0=ALU.mult, op1=ALU.add)
            else:
                nc.gpsimd.tensor_scalar(out=dst, in0=ns[:], scalar1=ec, scalar2=rc, op0=ALU.mult, op1=ALU.add)

        def rp_pe(b, a):
            if not ok(b):
                return
            T["rp", b, a] = psum.tile([P, DIM], F32, tag="rp", bufs=3, name="rp")
            for t in range(NT):
                nc.tensor.transpose(T["rp", b, a][:, t * P:(t + 1) * P], T["nrt", b][:, t, a * P:(a + 1) * P], ident[:])

        def evac_v(b, a):
            if not ok(b):
                return
            if a == 0:
                T["raw", b] = work.tile([P, NT, DIM], F32, tag="raw", bufs=3, name="raw_sb")
                T["mx", b] = small.tile([P, NT], F32, tag="mx", name="mx")
            nc.vector.tensor_scalar(out=T["raw", b][:, a, :], in0=T["rp", b, a][:], scalar1=-2.0, scalar2=None,
                                    op0=ALU.mult, op1=ALU.max, accum_out=T["mx", b][:, a:a + 1])

        def raw_store(b, a=None):
            if not ok(b):
                return
            if a is not None:
                nc.sync.dma_start(out=out_2[b].rearrange("(p a) i -> p a i", a=NT)[:, a, :], in_=T["raw", b][:, a, :])
                return
            nc.sync.dma_start(out=out_2[b].rearrange("(p a) i -> p (a i)", a=NT),
                              in_=T["raw", b][:].rearrange("p a i -> p (a i)"))

        def neg_s(b):
            if not ok(b):
                return
            T["nmx", b] = small.tile([P, NT], F32, tag="nmx", name="nmx")
            nc.scalar.mul(out=T["nmx", b][:], in_=T["mx", b][:], mul=-1.0)

        def exp_s(b, a):
            if not ok(b):
                return
            if a == 0:
                T["ex", b] = work.tile([P, NT, DIM], F32, tag="ex", bufs=3, name="ex")
                T["sm", b] = small.tile([P, NT], F32, tag="sm", name="sm")
            nc.scalar.activation(out=T["ex", b][:, a, :], in_=T["raw", b][:, a, :], func=ACT.Exp,
                                 bias=T["nmx", b][:, a:a + 1], scale=1.0, accum_out=T["sm", b][:, a:a + 1])

        def recip_v(b):
            if not ok(b):
                return
            T["rinv", b] = small.tile([P, NT], F32, tag="rinv", name="rinv")
            nc.vector.reciprocal(out=T["rinv", b][:], in_=T["sm", b][:])

        def p5(b, a):
            if not ok(b):
                return
            if a == 0:
                T["ph", b] = work.tile([P, NT, DIM], F32, tag="ph", bufs=3, name="ph")
            src, dst, rcp = T["ex", b][:, a, :], T["ph", b][:, a, :], T["rinv", b][:, a:a + 1]
            eng = p5_on(b)[a]
            if eng == "V":
                nc.vector.tensor_scalar_mul(out=dst, in0=src, scalar1=rcp)
            elif eng == "S":
                nc.scalar.activation(out=dst, in_=src, func=ACT.Copy, scale=rcp)
            else:
                nc.gpsimd.tensor_scalar(out=dst, in0=src, scalar1=rcp, scalar2=0.0, op0=ALU.mult, op1=ALU.add)

        def ph_store(b):
            if not ok(b):
                return
            nc.sync.dma_start(out=out_1[b].rearrange("(p a) i -> p (a i)", a=NT),
                              in_=T["ph", b][:].rearrange("p a i -> p (a i)"))

        def pt_pe(b, a):
            if not ok(b):
                return
            T["pt", b, a] = psum.tile([P, NT, P], F32, tag="pt", bufs=3, name="pt")
            for t in range(NT):
                nc.tensor.transpose(T["pt", b, a][:, t, :], T["ph", b][:, a, t * P:(t + 1) * P], ident[:])

        def pt_evac(b, a):
            if not ok(b):
                return
            if a == 0:
                T["gr", b] = work.tile([P, NT, P, NT], BF16, tag="gr", bufs=2, name="gr", align_bytes=64)
            src = T["pt", b, a][:].rearrange("q t p -> q p t")
            if pt_on(b)[a] == "S":
                nc.scalar.copy(out=T["gr", b][:, a], in_=src)
            else:
                nc.vector.tensor_copy(out=T["gr", b][:, a], in_=src)

        def quant_v(b):
            if not ok(b):
                return
            T["pc", b] = work.tile([P, DIM], U32, tag="pcodes", name="pcodes", align_bytes=64)
            T["ps", b] = work.tile([P, DIM], U8, tag="pscales", name="pscales", align_bytes=64)
            nc.vector.quantize_mx(out=T["pc", b][:].bitcast(FP8X4), scales=T["ps", b][:],
                                  in_=T["gr", b][:].rearrange("q a p t -> q (a p t)"))

        def mx_pe(b):
            if not ok(b):
                return
            T["op", b] = psum.tile([P, NT, Z], F32, tag="op", bufs=1, name="op")
            for a in range(NT):
                nc.tensor.matmul_mx(out=T["op", b][:, a, :],
                                    lhsT=T["pc", b][:, a * P:(a + 1) * P].bitcast(FP8X4),
                                    lhsT_scale=T["ps", b][:, a * P:(a + 1) * P],
                                    rhs=icodes[:, b, :].bitcast(FP8X4),
                                    rhs_scale=iscales[:, b, :],
                                    start=True, stop=True)

        def o_evac(b):
            if not ok(b):
                return
            osb = work.tile([P, NT, Z], F32, tag="osb", bufs=3, name="osb")
            if b < OTAIL:
                nc.scalar.copy(out=osb[:], in_=T["op", b][:])
            else:
                nc.vector.tensor_copy(out=osb[:], in_=T["op", b][:])
            nc.sync.dma_start(out=out_0[b].rearrange("(p a) z -> p (a z)", a=NT),
                              in_=osb[:].rearrange("p a z -> p (a z)"))

        for t in range(NT):
            cmp_v(0, t)
        for a in range(NT):
            row_pe(0, a)
        for t in range(NT):
            cmp_v(1, t)
        row_v(0)
        row_g(0)
        for t in range(NT):
            rawt_g(0, t)
        in_regroup(0)
        in_regroup(1)
        for a in range(NT):
            row_pe(1, a)
        for t in range(NT):
            cmp_v(2, t)
        row_v(1)
        row_g(1)
        for k in range(1, B + 6):
            for x in range(NT):
                if x == 0:
                    recip_v(k - 3)
                    for t in range(NT):
                        rawt_g(k, t)
                rp_pe(k - 1, x)
                pt_pe(k - 4, x)
                evac_v(k - 1, x)
                if k == 1:
                    raw_store(0, x)
                exp_s(k - 2, x)
                pt_evac(k - 4, x)
                if x == 0:
                    quant_v(k - 5)
                    for a in range(NT):
                        p5(k - 3, a)
                    for t in range(NT):
                        cmp_v(k + 2, t)
                    if k in (4, 8):
                        in_regroup(2 + (k == 8))
                    if k in (2, 3, 5, 9):
                        in_quant((2, 3, 5, 9).index(k))
                if x == 1:
                    for a in range(NT):
                        row_pe(k + 1, a)
                if x == 2:
                    mx_pe(k - 5)
                if x == 2:
                    row_v(k + 1)
                    row_g(k + 1)
            neg_s(k - 1)
            if k != 1:
                raw_store(k - 1)
            ph_store(k - 3)
            o_evac(k - 5)
